import numpy as np
import ml_dtypes


def mxq(x, axis, fmt="e4m3"):
    dtype, down = {"e4m3": (ml_dtypes.float8_e4m3fn, 7), "e5m2": (ml_dtypes.float8_e5m2, 14)}[fmt]
    v = np.moveaxis(np.asarray(x, np.float32).astype(ml_dtypes.bfloat16).astype(np.float64), axis, -1)
    blocks = v.reshape(v.shape[:-1] + (-1, 32))
    amax = np.abs(blocks).max(-1, keepdims=True)
    byte = np.maximum(np.where(amax > 0, np.frexp(amax)[1] - 1 + 127, 0) - down, 1)
    scale = np.exp2(byte - 127.0)
    codes = (blocks / scale).astype(np.float32).astype(dtype).astype(np.float64)
    return np.moveaxis((codes * scale).reshape(v.shape), -1, axis)


WIDE = False


def mx_kscale(k):
    if not WIDE:
        return np.ones(k)
    levels = np.array([10, -10, 5, -5, 0])
    a = np.random.permutation(np.resize(levels, k // 512 * 4)).reshape(k // 512, 4)
    idx = np.arange(k)
    return np.exp2(a[idx // 512, idx % 128 // 32])


BF16 = ml_dtypes.bfloat16


def bf(x):
    return np.asarray(x, np.float32).astype(BF16)


def f64(x):
    return np.asarray(x).astype(np.float64)


E2M1 = np.array([0.0, 0.5, 1.0, 1.5, 2.0, 3.0, 4.0, 6.0, -0.0, -0.5, -1.0, -1.5, -2.0, -3.0, -4.0, -6.0])


def pack_weight(w, fmt):
    k, n = w.shape
    w = f64(bf(w)).reshape(k // 32, 32, n)
    amax = np.abs(w).max(1)
    if fmt == "e4m3":
        byte = np.frexp(amax)[1] - 1 + 127 - 7
    else:
        mant, ex = np.frexp(amax / 6.0)
        byte = np.where(mant > 0.5, ex, ex - 1) + 127
    byte = np.clip(np.where(amax > 0, byte, 1), 1, 254)
    scaled = (w * np.exp2(127.0 - byte)[:, None, :]).reshape(k, n).astype(np.float32)
    by_word = np.ascontiguousarray(scaled.reshape(k // 512, 128, 4, n).transpose(0, 1, 3, 2))
    if fmt == "e4m3":
        words = by_word.astype(ml_dtypes.float8_e4m3fn).view(np.uint8)
    else:
        c = by_word.astype(ml_dtypes.float4_e2m1fn).view(np.uint8) & 0xF
        words = c[..., 0::2] | (c[..., 1::2] << 4)
    return np.ascontiguousarray(words), np.ascontiguousarray(byte.astype(np.uint8).reshape(k // 512, 16, n))


def unpack_weight(words, scales, fmt):
    g, p, n, _ = words.shape
    if fmt == "e4m3":
        vals = np.ascontiguousarray(words).view(ml_dtypes.float8_e4m3fn).astype(np.float64)
    else:
        nib = np.empty((g, p, n, 4), np.uint8)
        nib[..., 0::2] = words & 0xF
        nib[..., 1::2] = words >> 4
        vals = E2M1[nib]
    vals = vals * np.repeat(np.exp2(scales.astype(np.float64) - 127.0), 8, axis=1)[..., None]
    return vals.transpose(0, 1, 3, 2).reshape(g * 512, n)


M, I0, I1, I2, N0, N1, N2 = 128, 1024, 2048, 4096, 2048, 2048, 4608
FMT = "e4m3"


def block(fan_in, fan_out, s):
    return pack_weight(np.random.uniform(-1.0, 1.0, (fan_in, fan_out)) / np.sqrt(fan_in) / s[:fan_in, None], FMT)


def setup_inputs():
    s = mx_kscale(I2)
    x = bf(np.random.standard_normal((M, I2)) * s)
    w0_words, w0_scales = block(I0, N0, s)
    w1_words, w1_scales = block(I1, N1, s)
    w2_words, w2_scales = block(I2, N2, s)
    bias = bf(np.random.standard_normal(N0 + N1 + N2) * 0.1)
    return {"x": x,
            "w0_words": w0_words, "w0_scales": w0_scales,
            "w1_words": w1_words, "w1_scales": w1_scales,
            "w2_words": w2_words, "w2_scales": w2_scales,
            "bias": bias}


def reference(x, w0_words, w0_scales, w1_words, w1_scales, w2_words, w2_scales, bias):
    xq = mxq(f64(x), 1, "e4m3")
    y0 = xq[:, :I0] @ unpack_weight(w0_words, w0_scales, FMT)
    y1 = xq[:, :I1] @ unpack_weight(w1_words, w1_scales, FMT)
    y2 = xq[:, :I2] @ unpack_weight(w2_words, w2_scales, FMT)
    return np.concatenate([y0, y1, y2], axis=1) + f64(bias)

@@ -1,0 +1,180 @@
+from contextlib import ExitStack
+
+import concourse.mybir as mybir
+from concourse.masks import make_identity
+
+F32 = mybir.dt.float32
+BF16 = mybir.dt.bfloat16
+I32 = mybir.dt.int32
+U32 = mybir.dt.uint32
+U8 = mybir.dt.uint8
+FP8X4 = mybir.dt.float8_e4m3fn_x4
+ADD = mybir.AluOpType.add
+
+P = 128
+K_PASS = 512
+BANK = 512
+K_X = 4096
+N0, N1, N2 = 2048, 2048, 4608
+N_OUT = N0 + N1 + N2
+FLOPS = 2 * 128 * (1024 * N0 + 2048 * N1 + 4096 * N2)
+
+OFF_W0 = 0
+OFF_W1 = N0
+OFF_W2A = N0 + N1
+OFF_W2B = N0 + N1 + N2
+PLANE_COLS = N0 + N1 + 2 * N2
+
+
+def tile_mlinear_w_kernel(
+    tc, x, w0_words, w0_scales, w1_words, w1_scales, w2_words, w2_scales, bias, out
+):
+    nc = tc.nc
+    with ExitStack() as ctx:
+        keep = ctx.enter_context(tc.tile_pool(name="keep", bufs=1))
+        slabs = ctx.enter_context(tc.tile_pool(name="slabs", bufs=9))
+        psum = ctx.enter_context(tc.psum_pool(name="psum", bufs=8))
+        ctx.enter_context(tc.manual_schedule())
+
+        def bank(name):
+            return psum.tile([P, BANK], F32, tag="bank", name=name)
+
+        ident_f32 = keep.tile([P, P], F32, name="ident_f32")
+        make_identity(nc, ident_f32[:])
+        ident_bf = keep.tile([P, P], BF16, name="ident_bf")
+        make_identity(nc, ident_bf[:])
+
+        bias_rows = keep.tile([P, BANK], BF16, name="bias_rows")
+        nc.vector.memset(bias_rows[:], 0.0)
+        planes = keep.tile([P, PLANE_COLS], U8, name="planes", align_bytes=64)
+        for lo, hi in ((OFF_W0, OFF_W1), (OFF_W1, OFF_W2A), (OFF_W2A, OFF_W2B), (OFF_W2B, PLANE_COLS)):
+            nc.vector.memset(planes[:, lo:hi].bitcast(I32), 0)
+
+        n_bias = N_OUT // BANK
+        nc.scalar.dma_start(out=bias_rows[0:n_bias, :], in_=bias.rearrange("(j n) -> j n", n=BANK))
+
+        x_sb = slabs.tile([P, K_X], BF16, tag="slab", name="x_sb", align_bytes=64)
+        half = K_X // 2
+        for h in range(2):
+            nc.sync.dma_start(out=x_sb[:, h * half:(h + 1) * half], in_=x[:, h * half:(h + 1) * half])
+        grouped = slabs.tile([P, K_X], BF16, tag="slab", name="grouped", align_bytes=64)
+
+        def load_planes(scales, g0, n_planes, off, width):
+            for q in range(4):
+                nc.sync.dma_start(
+                    out=planes[32 * q:32 * q + 4 * n_planes, off:off + width].bitcast(I32),
+                    in_=scales[g0:g0 + n_planes, 4 * q:4 * q + 4, :].bitcast(I32),
+                )
+
+        load_planes(w0_scales, 0, 2, OFF_W0, N0)
+        load_planes(w1_scales, 0, 4, OFF_W1, N1)
+        load_planes(w2_scales, 0, 4, OFF_W2A, N2)
+        load_planes(w2_scales, 4, 4, OFF_W2B, N2)
+
+        def load_pair(words, g0, name):
+            t = slabs.tile([P, 2, N0], U32, tag="slab", name=name, align_bytes=64)
+            nc.sync.dma_start(
+                out=t[:].bitcast(I32),
+                in_=words[g0:g0 + 2].rearrange("g p n t -> p g (n t)").bitcast(I32),
+            )
+            return t
+
+        def load_w2(g):
+            t = slabs.tile([P, N2], U32, tag="slab", name="w2_g%d" % g, align_bytes=64)
+            nc.sync.dma_start(
+                out=t[:].bitcast(I32),
+                in_=w2_words[g].rearrange("p n t -> p (n t)").bitcast(I32),
+            )
+            return t
+
+        w0_t = load_pair(w0_words, 0, "w0_t")
+        w1_a = load_pair(w1_words, 0, "w1_a")
+        w1_b = load_pair(w1_words, 2, "w1_b")
+        w2_t = [load_w2(g) for g in range(4)]
+
+        xq = keep.tile([P, K_X // 4], U32, name="xq", align_bytes=64)
+        xs = keep.tile([P, K_X // 4], U8, name="xs", align_bytes=64)
+        x_words = x_sb[:].bitcast(F32)
+        grouped_words = grouped[:].bitcast(F32)
+        xt = []
+        for b in range(4):
+            t = bank("xt%d" % b)
+            for gl in range(2):
+                g = 2 * b + gl
+                for u in range(2):
+                    c = (2 * gl + u) * P
+                    nc.tensor.transpose(t[:, c:c + P], x_words[:, 256 * g + u:256 * (g + 1):2], ident_f32[:])
+            xt.append(t)
+        for b in (0, 2, 1, 3):
+            dst = grouped_words[:, BANK * b:BANK * (b + 1)].rearrange("p (g m u) -> p g m u", g=2, u=2)
+            src = xt[b][:].rearrange("p (g u m) -> p g m u", g=2, u=2)
+            if b % 2 == 0:
+                nc.vector.tensor_copy(out=dst, in_=src)
+            else:
+                nc.scalar.copy(out=dst, in_=src)
+        for b in range(4):
+            nc.vector.quantize_mx(
+                out=xq[:, 256 * b:256 * (b + 1)].bitcast(FP8X4),
+                scales=xs[:, 256 * b:256 * (b + 1)],
+                in_=grouped[:, 1024 * b:1024 * (b + 1)],
+            )
+
+        out_sb = keep.tile([P, N_OUT], F32, name="out_sb")
+        for j in range(n_bias):
+            t = bank("bias%d" % j)
+            nc.tensor.matmul(
+                out=t[:], lhsT=ident_bf[:, j:j + 1].to_broadcast([P, P]), rhs=bias_rows[:], start=True, stop=True
+            )
+            nc.scalar.copy(out=out_sb[:, BANK * j:BANK * (j + 1)], in_=t[:])
+
+        w2_t.append(load_w2(4))
+        w2_t.append(load_w2(5))
+
+        def mx_pass(acc, g, n_groups, words, k_plane, plane_col):
+            nc.tensor.matmul_mx(
+                out=acc[:],
+                lhsT=xq[:, P * g:P * (g + 1)].bitcast(FP8X4),
+                lhsT_scale=xs[:, P * g:P * (g + 1)],
+                rhs=words.bitcast(FP8X4),
+                rhs_scale=planes[k_plane:P, plane_col:plane_col + BANK],
+                start=(g == 0),
+                stop=(g == n_groups - 1),
+            )
+
+        def add_bias(acc, col):
+            nc.vector.tensor_tensor(out=out_sb[:, col:col + BANK], in0=acc[:], in1=out_sb[:, col:col + BANK], op=ADD)
+
+        acc0 = [bank("acc0_%d" % j) for j in range(4)]
+        for g in range(2):
+            for j in range(4):
+                mx_pass(acc0[j], g, 2, w0_t[:, g, BANK * j:BANK * (j + 1)], 4 * g, OFF_W0 + BANK * j)
+        for j in range(4):
+            add_bias(acc0[j], BANK * j)
+        w2_t.append(load_w2(6))
+
+        acc1 = [bank("acc1_%d" % j) for j in range(4)]
+        for g in range(4):
+            src_t = w1_a if g < 2 else w1_b
+            for j in range(4):
+                mx_pass(acc1[j], g, 4, src_t[:, g % 2, BANK * j:BANK * (j + 1)], 4 * g, OFF_W1 + BANK * j)
+        for j in range(4):
+            add_bias(acc1[j], N0 + BANK * j)
+        w2_t.append(load_w2(7))
+
+        def w2_pass(acc, g, j):
+            off = OFF_W2A if g < 4 else OFF_W2B
+            mx_pass(acc, g, 8, w2_t[g][:, BANK * j:BANK * (j + 1)], 4 * (g % 4), off + BANK * j)
+
+        acc2 = [bank("acc2_%d" % j) for j in range(8)]
+        for g in range(8):
+            for j in range(8):
+                w2_pass(acc2[j], g, j)
+        for j in range(8):
+            add_bias(acc2[j], N0 + N1 + BANK * j)
+        acc_last = bank("acc2_8")
+        for g in range(8):
+            w2_pass(acc_last, g, 8)
+        add_bias(acc_last, N0 + N1 + BANK * 8)
+
+        for lo, hi in ((0, 4096), (4096, 6144), (6144, 8192), (8192, 8704)):
+            nc.sync.dma_start(out=out[:, lo:hi], in_=out_sb[:, lo:hi])

@@ -60,10 +60,10 @@ def tile_mlinear_w_kernel(
         grouped = slabs.tile([P, K_X], BF16, tag="slab", name="grouped", align_bytes=64)
 
         def load_planes(scales, g0, n_planes, off, width):
-            for q in range(4):
-                nc.sync.dma_start(
-                    out=planes[32 * q:32 * q + 4 * n_planes, off:off + width].bitcast(I32),
-                    in_=scales[g0:g0 + n_planes, 4 * q:4 * q + 4, :].bitcast(I32),
+            for q in (0, 2, 1, 3):
+                nc.gpsimd.dma_start(
+                    out=planes[32 * q:32 * q + 4 * n_planes, off:off + width].bitcast(F32),
+                    in_=scales[g0:g0 + n_planes, 4 * q:4 * q + 4, :].bitcast(F32),
                 )
 
         load_planes(w0_scales, 0, 2, OFF_W0, N0)

@@ -79,12 +79,13 @@ def tile_mlinear_w_kernel(
             )
             return t
 
-        def load_w2(g):
+        def load_w2(g, cuts=(0, N2)):
             t = slabs.tile([P, N2], U32, tag="slab", name="w2_g%d" % g, align_bytes=64)
-            nc.sync.dma_start(
-                out=t[:].bitcast(I32),
-                in_=w2_words[g].rearrange("p n t -> p (n t)").bitcast(I32),
-            )
+            for lo, hi in zip(cuts[:-1], cuts[1:]):
+                nc.sync.dma_start(
+                    out=t[:, lo:hi].bitcast(I32),
+                    in_=w2_words[g, :, lo:hi, :].rearrange("p n t -> p (n t)").bitcast(I32),
+                )
             return t
 
         w0_t = load_pair(w0_words, 0, "w0_t")
@@ -159,22 +160,29 @@ def tile_mlinear_w_kernel(
                 mx_pass(acc1[j], g, 4, src_t[:, g % 2, BANK * j:BANK * (j + 1)], 4 * g, OFF_W1 + BANK * j)
         for j in range(4):
             add_bias(acc1[j], N0 + BANK * j)
-        w2_t.append(load_w2(7))
+        w2_t.append(load_w2(7, (0, 2048, 4096, N2)))
 
         def w2_pass(acc, g, j):
             off = OFF_W2A if g < 4 else OFF_W2B
             mx_pass(acc, g, 8, w2_t[g][:, BANK * j:BANK * (j + 1)], 4 * (g % 4), off + BANK * j)
 
         acc2 = [bank("acc2_%d" % j) for j in range(8)]
-        for g in range(8):
+        for g in range(7):
             for j in range(8):
                 w2_pass(acc2[j], g, j)
-        for j in range(8):
+        for j in range(4):
+            w2_pass(acc2[j], 7, j)
+        for j in range(4):
             add_bias(acc2[j], N0 + N1 + BANK * j)
         acc_last = bank("acc2_8")
-        for g in range(8):
+        for g in range(7):
             w2_pass(acc_last, g, 8)
+        for j in range(4, 8):
+            w2_pass(acc2[j], 7, j)
+        w2_pass(acc_last, 7, 8)
+        for j in range(4, 8):
+            add_bias(acc2[j], N0 + N1 + BANK * j)
         add_bias(acc_last, N0 + N1 + BANK * 8)
 
-        for lo, hi in ((0, 4096), (4096, 6144), (6144, 8192), (8192, 8704)):
+        for lo, hi in ((0, 4096), (4096, 6144), (6144, 8704)):
             nc.sync.dma_start(out=out[:, lo:hi], in_=out_sb[:, lo:hi])

@@ -60,16 +60,14 @@ def tile_mlinear_w_kernel(
         grouped = slabs.tile([P, K_X], BF16, tag="slab", name="grouped", align_bytes=64)
 
         def load_planes(scales, g0, n_planes, off, width):
-            for q in (0, 2, 1, 3):
-                nc.gpsimd.dma_start(
+            for q, queue in ((0, nc.scalar), (2, nc.gpsimd), (1, nc.scalar), (3, nc.gpsimd)):
+                queue.dma_start(
                     out=planes[32 * q:32 * q + 4 * n_planes, off:off + width].bitcast(F32),
                     in_=scales[g0:g0 + n_planes, 4 * q:4 * q + 4, :].bitcast(F32),
                 )
 
         load_planes(w0_scales, 0, 2, OFF_W0, N0)
         load_planes(w1_scales, 0, 4, OFF_W1, N1)
-        load_planes(w2_scales, 0, 4, OFF_W2A, N2)
-        load_planes(w2_scales, 4, 4, OFF_W2B, N2)
 
         def load_pair(words, g0, name):
             t = slabs.tile([P, 2, N0], U32, tag="slab", name=name, align_bytes=64)
@@ -91,6 +89,7 @@ def tile_mlinear_w_kernel(
         w0_t = load_pair(w0_words, 0, "w0_t")
         w1_a = load_pair(w1_words, 0, "w1_a")
         w1_b = load_pair(w1_words, 2, "w1_b")
+        load_planes(w2_scales, 0, 4, OFF_W2A, N2)
         w2_t = [load_w2(g) for g in range(4)]
 
         xq = keep.tile([P, K_X // 4], U32, name="xq", align_bytes=64)
@@ -128,6 +127,7 @@ def tile_mlinear_w_kernel(
             )
             nc.scalar.copy(out=out_sb[:, BANK * j:BANK * (j + 1)], in_=t[:])
 
+        load_planes(w2_scales, 4, 4, OFF_W2B, N2)
         w2_t.append(load_w2(4))
         w2_t.append(load_w2(5))
 

@@ -51,7 +51,9 @@ def tile_mlinear_w_kernel(
             nc.vector.memset(planes[:, lo:hi].bitcast(I32), 0)
 
         n_bias = N_OUT // BANK
-        nc.scalar.dma_start(out=bias_rows[0:n_bias, :], in_=bias.rearrange("(j n) -> j n", n=BANK))
+        bias_by_row = bias.rearrange("(j n) -> j n", n=BANK)
+        nc.scalar.dma_start(out=bias_rows[0:16, :], in_=bias_by_row[0:16, :])
+        nc.scalar.dma_start(out=bias_rows[16:n_bias, :], in_=bias_by_row[16:n_bias, :])
 
         x_sb = slabs.tile([P, K_X], BF16, tag="slab", name="x_sb", align_bytes=64)
         half = K_X // 2
@@ -67,7 +69,6 @@ def tile_mlinear_w_kernel(
                 )
 
         load_planes(w0_scales, 0, 2, OFF_W0, N0)
-        load_planes(w1_scales, 0, 4, OFF_W1, N1)
 
         def load_pair(words, g0, name):
             t = slabs.tile([P, 2, N0], U32, tag="slab", name=name, align_bytes=64)
@@ -88,6 +89,7 @@ def tile_mlinear_w_kernel(
 
         w0_t = load_pair(w0_words, 0, "w0_t")
         w1_a = load_pair(w1_words, 0, "w1_a")
+        load_planes(w1_scales, 0, 4, OFF_W1, N1)
         w1_b = load_pair(w1_words, 2, "w1_b")
         load_planes(w2_scales, 0, 4, OFF_W2A, N2)
         w2_t = [load_w2(g) for g in range(4)]

@@ -61,14 +61,30 @@ def tile_mlinear_w_kernel(
             nc.sync.dma_start(out=x_sb[:, h * half:(h + 1) * half], in_=x[:, h * half:(h + 1) * half])
         grouped = slabs.tile([P, K_X], BF16, tag="slab", name="grouped", align_bytes=64)
 
+        def load_quadrant(queue, q, scales, g0, n_planes, off, lo, hi):
+            queue.dma_start(
+                out=planes[32 * q:32 * q + 4 * n_planes, off + lo:off + hi].bitcast(F32),
+                in_=scales[g0:g0 + n_planes, 4 * q:4 * q + 4, lo:hi].bitcast(F32),
+            )
+
         def load_planes(scales, g0, n_planes, off, width):
-            for q, queue in ((0, nc.scalar), (2, nc.gpsimd), (1, nc.scalar), (3, nc.gpsimd)):
-                queue.dma_start(
-                    out=planes[32 * q:32 * q + 4 * n_planes, off:off + width].bitcast(F32),
-                    in_=scales[g0:g0 + n_planes, 4 * q:4 * q + 4, :].bitcast(F32),
-                )
+            for q in (0, 1):
+                load_quadrant(nc.scalar, q, scales, g0, n_planes, off, 0, width)
 
         load_planes(w0_scales, 0, 2, OFF_W0, N0)
+        half_n1 = N1 // 2
+        for q, scales, g0, n_planes, off, lo, hi in (
+            (2, w0_scales, 0, 2, OFF_W0, 0, N0),
+            (3, w0_scales, 0, 2, OFF_W0, 0, N0),
+            (3, w1_scales, 0, 4, OFF_W1, 0, N1),
+            (2, w2_scales, 0, 4, OFF_W2A, 0, N2),
+            (2, w1_scales, 0, 4, OFF_W1, 0, half_n1),
+            (2, w1_scales, 0, 4, OFF_W1, half_n1, N1),
+            (3, w2_scales, 0, 4, OFF_W2A, 0, N2),
+            (2, w2_scales, 4, 4, OFF_W2B, 0, N2),
+            (3, w2_scales, 4, 4, OFF_W2B, 0, N2),
+        ):
+            load_quadrant(nc.gpsimd, q, scales, g0, n_planes, off, lo, hi)
 
         def load_pair(words, g0, name):
             t = slabs.tile([P, 2, N0], U32, tag="slab", name=name, align_bytes=64)

@@ -56,9 +56,7 @@ def tile_mlinear_w_kernel(
         nc.scalar.dma_start(out=bias_rows[16:n_bias, :], in_=bias_by_row[16:n_bias, :])
 
         x_sb = slabs.tile([P, K_X], BF16, tag="slab", name="x_sb", align_bytes=64)
-        half = K_X // 2
-        for h in range(2):
-            nc.sync.dma_start(out=x_sb[:, h * half:(h + 1) * half], in_=x[:, h * half:(h + 1) * half])
+        nc.sync.dma_start(out=x_sb[:], in_=x)
         grouped = slabs.tile([P, K_X], BF16, tag="slab", name="grouped", align_bytes=64)
 
         def load_quadrant(queue, q, scales, g0, n_planes, off, lo, hi):
@@ -72,14 +70,14 @@ def tile_mlinear_w_kernel(
                 load_quadrant(nc.scalar, q, scales, g0, n_planes, off, 0, width)
 
         load_planes(w0_scales, 0, 2, OFF_W0, N0)
-        half_n1 = N1 // 2
+        cut = 64
         for q, scales, g0, n_planes, off, lo, hi in (
             (2, w0_scales, 0, 2, OFF_W0, 0, N0),
             (3, w0_scales, 0, 2, OFF_W0, 0, N0),
             (3, w1_scales, 0, 4, OFF_W1, 0, N1),
             (2, w2_scales, 0, 4, OFF_W2A, 0, N2),
-            (2, w1_scales, 0, 4, OFF_W1, 0, half_n1),
-            (2, w1_scales, 0, 4, OFF_W1, half_n1, N1),
+            (2, w1_scales, 0, 4, OFF_W1, cut, N1),
+            (2, w1_scales, 0, 4, OFF_W1, 0, cut),
             (3, w2_scales, 0, 4, OFF_W2A, 0, N2),
             (2, w2_scales, 4, 4, OFF_W2B, 0, N2),
             (3, w2_scales, 4, 4, OFF_W2B, 0, N2),
@@ -178,7 +176,7 @@ def tile_mlinear_w_kernel(
                 mx_pass(acc1[j], g, 4, src_t[:, g % 2, BANK * j:BANK * (j + 1)], 4 * g, OFF_W1 + BANK * j)
         for j in range(4):
             add_bias(acc1[j], N0 + BANK * j)
-        w2_t.append(load_w2(7, (0, 2048, 4096, N2)))
+        w2_t.append(load_w2(7, (0, 2048, N2)))
 
         def w2_pass(acc, g, j):
             off = OFF_W2A if g < 4 else OFF_W2B

@@ -61,15 +61,14 @@ def tile_mlinear_w_kernel(
 
         def load_quadrant(queue, q, scales, g0, n_planes, off, lo, hi):
             queue.dma_start(
-                out=planes[32 * q:32 * q + 4 * n_planes, off + lo:off + hi].bitcast(F32),
-                in_=scales[g0:g0 + n_planes, 4 * q:4 * q + 4, lo:hi].bitcast(F32),
+                out=planes[32 * q:32 * q + 4 * n_planes, off + lo:off + hi].bitcast(I32),
+                in_=scales[g0:g0 + n_planes, 4 * q:4 * q + 4, lo:hi].bitcast(I32),
             )
 
         def load_planes(scales, g0, n_planes, off, width):
             for q in (0, 1):
-                load_quadrant(nc.scalar, q, scales, g0, n_planes, off, 0, width)
+                load_quadrant(nc.sync, q, scales, g0, n_planes, off, 0, width)
 
-        load_planes(w0_scales, 0, 2, OFF_W0, N0)
         cut = 64
         for q, scales, g0, n_planes, off, lo, hi in (
             (2, w0_scales, 0, 2, OFF_W0, 0, N0),
@@ -102,10 +101,12 @@ def tile_mlinear_w_kernel(
             return t
 
         w0_t = load_pair(w0_words, 0, "w0_t")
-        w1_a = load_pair(w1_words, 0, "w1_a")
+        load_planes(w0_scales, 0, 2, OFF_W0, N0)
         load_planes(w1_scales, 0, 4, OFF_W1, N1)
-        w1_b = load_pair(w1_words, 2, "w1_b")
         load_planes(w2_scales, 0, 4, OFF_W2A, N2)
+        w1_a = load_pair(w1_words, 0, "w1_a")
+        w1_b = load_pair(w1_words, 2, "w1_b")
+        load_planes(w2_scales, 4, 4, OFF_W2B, N2)
         w2_t = [load_w2(g) for g in range(4)]
 
         xq = keep.tile([P, K_X // 4], U32, name="xq", align_bytes=64)
@@ -143,7 +144,6 @@ def tile_mlinear_w_kernel(
             )
             nc.scalar.copy(out=out_sb[:, BANK * j:BANK * (j + 1)], in_=t[:])
 
-        load_planes(w2_scales, 4, 4, OFF_W2B, N2)
         w2_t.append(load_w2(4))
         w2_t.append(load_w2(5))
 

@@ -176,7 +176,7 @@ def tile_mlinear_w_kernel(
                 mx_pass(acc1[j], g, 4, src_t[:, g % 2, BANK * j:BANK * (j + 1)], 4 * g, OFF_W1 + BANK * j)
         for j in range(4):
             add_bias(acc1[j], N0 + BANK * j)
-        w2_t.append(load_w2(7, (0, 2048, N2)))
+        w2_t.append(load_w2(7, (0, 2048, 3584, N2)))
 
         def w2_pass(acc, g, j):
             off = OFF_W2A if g < 4 else OFF_W2B
@@ -190,15 +190,16 @@ def tile_mlinear_w_kernel(
             w2_pass(acc2[j], 7, j)
         for j in range(4):
             add_bias(acc2[j], N0 + N1 + BANK * j)
+        for j in range(4, 7):
+            w2_pass(acc2[j], 7, j)
         acc_last = bank("acc2_8")
         for g in range(7):
             w2_pass(acc_last, g, 8)
-        for j in range(4, 8):
-            w2_pass(acc2[j], 7, j)
+        w2_pass(acc2[7], 7, 7)
         w2_pass(acc_last, 7, 8)
         for j in range(4, 8):
             add_bias(acc2[j], N0 + N1 + BANK * j)
         add_bias(acc_last, N0 + N1 + BANK * 8)
 
-        for lo, hi in ((0, 4096), (4096, 6144), (6144, 8704)):
+        for lo, hi in ((0, 4096), (4096, 7168), (7168, 8704)):
             nc.sync.dma_start(out=out[:, lo:hi], in_=out_sb[:, lo:hi])

@@ -46,7 +46,7 @@ def tile_mlinear_w_kernel(
 
         bias_rows = keep.tile([P, BANK], BF16, name="bias_rows")
         nc.vector.memset(bias_rows[:], 0.0)
-        planes = keep.tile([P, PLANE_COLS], U8, name="planes", align_bytes=64)
+        planes = keep.tile([P, PLANE_COLS], U8, name="planes", align_bytes=256)
         for lo, hi in ((OFF_W0, OFF_W1), (OFF_W1, OFF_W2A), (OFF_W2A, OFF_W2B), (OFF_W2B, PLANE_COLS)):
             nc.vector.memset(planes[:, lo:hi].bitcast(I32), 0)
 
@@ -55,9 +55,9 @@ def tile_mlinear_w_kernel(
         nc.scalar.dma_start(out=bias_rows[0:16, :], in_=bias_by_row[0:16, :])
         nc.scalar.dma_start(out=bias_rows[16:n_bias, :], in_=bias_by_row[16:n_bias, :])
 
-        x_sb = slabs.tile([P, K_X], BF16, tag="slab", name="x_sb", align_bytes=64)
+        x_sb = slabs.tile([P, K_X], BF16, tag="slab", name="x_sb", align_bytes=256)
         nc.sync.dma_start(out=x_sb[:], in_=x)
-        grouped = slabs.tile([P, K_X], BF16, tag="slab", name="grouped", align_bytes=64)
+        grouped = slabs.tile([P, K_X], BF16, tag="slab", name="grouped", align_bytes=256)
 
         def load_quadrant(queue, q, scales, g0, n_planes, off, lo, hi):
             queue.dma_start(
@@ -84,7 +84,7 @@ def tile_mlinear_w_kernel(
             load_quadrant(nc.gpsimd, q, scales, g0, n_planes, off, lo, hi)
 
         def load_pair(words, g0, name):
-            t = slabs.tile([P, 2, N0], U32, tag="slab", name=name, align_bytes=64)
+            t = slabs.tile([P, 2, N0], U32, tag="slab", name=name, align_bytes=256)
             nc.sync.dma_start(
                 out=t[:].bitcast(I32),
                 in_=words[g0:g0 + 2].rearrange("g p n t -> p g (n t)").bitcast(I32),
@@ -92,7 +92,7 @@ def tile_mlinear_w_kernel(
             return t
 
         def load_w2(g, cuts=(0, N2)):
-            t = slabs.tile([P, N2], U32, tag="slab", name="w2_g%d" % g, align_bytes=64)
+            t = slabs.tile([P, N2], U32, tag="slab", name="w2_g%d" % g, align_bytes=256)
             for lo, hi in zip(cuts[:-1], cuts[1:]):
                 nc.sync.dma_start(
                     out=t[:, lo:hi].bitcast(I32),
@@ -109,8 +109,8 @@ def tile_mlinear_w_kernel(
         load_planes(w2_scales, 4, 4, OFF_W2B, N2)
         w2_t = [load_w2(g) for g in range(4)]
 
-        xq = keep.tile([P, K_X // 4], U32, name="xq", align_bytes=64)
-        xs = keep.tile([P, K_X // 4], U8, name="xs", align_bytes=64)
+        xq = keep.tile([P, K_X // 4], U32, name="xq", align_bytes=256)
+        xs = keep.tile([P, K_X // 4], U8, name="xs", align_bytes=256)
         x_words = x_sb[:].bitcast(F32)
         grouped_words = grouped[:].bitcast(F32)
         xt = []
@@ -136,7 +136,7 @@ def tile_mlinear_w_kernel(
                 in_=grouped[:, 1024 * b:1024 * (b + 1)],
             )
 
-        out_sb = keep.tile([P, N_OUT], F32, name="out_sb")
+        out_sb = keep.tile([P, N_OUT], F32, name="out_sb", align_bytes=256)
         for j in range(n_bias):
             t = bank("bias%d" % j)
             nc.tensor.matmul(

from contextlib import ExitStack

import concourse.mybir as mybir
from concourse.masks import make_identity

F32 = mybir.dt.float32
BF16 = mybir.dt.bfloat16
I32 = mybir.dt.int32
U32 = mybir.dt.uint32
U8 = mybir.dt.uint8
FP8X4 = mybir.dt.float8_e4m3fn_x4
ADD = mybir.AluOpType.add

P = 128
K_PASS = 512
BANK = 512
K_X = 4096
N0, N1, N2 = 2048, 2048, 4608
N_OUT = N0 + N1 + N2
FLOPS = 2 * 128 * (1024 * N0 + 2048 * N1 + 4096 * N2)

OFF_W0 = 0
OFF_W1 = N0
OFF_W2A = N0 + N1
OFF_W2B = N0 + N1 + N2
PLANE_COLS = N0 + N1 + 2 * N2


def tile_mlinear_w_kernel(
    tc, x, w0_words, w0_scales, w1_words, w1_scales, w2_words, w2_scales, bias, out
):
    nc = tc.nc
    with ExitStack() as ctx:
        keep = ctx.enter_context(tc.tile_pool(name="keep", bufs=1))
        slabs = ctx.enter_context(tc.tile_pool(name="slabs", bufs=9))
        psum = ctx.enter_context(tc.psum_pool(name="psum", bufs=8))
        ctx.enter_context(tc.manual_schedule())

        def bank(name):
            return psum.tile([P, BANK], F32, tag="bank", name=name)

        ident_f32 = keep.tile([P, P], F32, name="ident_f32")
        make_identity(nc, ident_f32[:])
        ident_bf = keep.tile([P, P], BF16, name="ident_bf")
        make_identity(nc, ident_bf[:])

        bias_rows = keep.tile([P, BANK], BF16, name="bias_rows")
        nc.vector.memset(bias_rows[:], 0.0)
        planes = keep.tile([P, PLANE_COLS], U8, name="planes", align_bytes=256)
        for lo, hi in ((OFF_W0, OFF_W1), (OFF_W1, OFF_W2A), (OFF_W2A, OFF_W2B), (OFF_W2B, PLANE_COLS)):
            nc.vector.memset(planes[:, lo:hi].bitcast(I32), 0)

        n_bias = N_OUT // BANK
        bias_by_row = bias.rearrange("(j n) -> j n", n=BANK)
        nc.scalar.dma_start(out=bias_rows[0:16, :], in_=bias_by_row[0:16, :])
        nc.scalar.dma_start(out=bias_rows[16:n_bias, :], in_=bias_by_row[16:n_bias, :])

        x_sb = slabs.tile([P, K_X], BF16, tag="slab", name="x_sb", align_bytes=256)
        nc.sync.dma_start(out=x_sb[:], in_=x)
        grouped = slabs.tile([P, K_X], BF16, tag="slab", name="grouped", align_bytes=256)

        def load_quadrant(queue, q, scales, g0, n_planes, off, lo, hi):
            queue.dma_start(
                out=planes[32 * q:32 * q + 4 * n_planes, off + lo:off + hi].bitcast(I32),
                in_=scales[g0:g0 + n_planes, 4 * q:4 * q + 4, lo:hi].bitcast(I32),
            )

        def load_planes(scales, g0, n_planes, off, width):
            for q in (0, 1):
                load_quadrant(nc.sync, q, scales, g0, n_planes, off, 0, width)

        cut = 64
        for q, scales, g0, n_planes, off, lo, hi in (
            (2, w0_scales, 0, 2, OFF_W0, 0, N0),
            (3, w0_scales, 0, 2, OFF_W0, 0, N0),
            (3, w1_scales, 0, 4, OFF_W1, 0, N1),
            (2, w2_scales, 0, 4, OFF_W2A, 0, N2),
            (2, w1_scales, 0, 4, OFF_W1, cut, N1),
            (2, w1_scales, 0, 4, OFF_W1, 0, cut),
            (3, w2_scales, 0, 4, OFF_W2A, 0, N2),
            (2, w2_scales, 4, 4, OFF_W2B, 0, N2),
            (3, w2_scales, 4, 4, OFF_W2B, 0, N2),
        ):
            load_quadrant(nc.gpsimd, q, scales, g0, n_planes, off, lo, hi)

        def load_pair(words, g0, name):
            t = slabs.tile([P, 2, N0], U32, tag="slab", name=name, align_bytes=256)
            nc.sync.dma_start(
                out=t[:].bitcast(I32),
                in_=words[g0:g0 + 2].rearrange("g p n t -> p g (n t)").bitcast(I32),
            )
            return t

        def load_w2(g, cuts=(0, N2)):
            t = slabs.tile([P, N2], U32, tag="slab", name="w2_g%d" % g, align_bytes=256)
            for lo, hi in zip(cuts[:-1], cuts[1:]):
                nc.sync.dma_start(
                    out=t[:, lo:hi].bitcast(I32),
                    in_=w2_words[g, :, lo:hi, :].rearrange("p n t -> p (n t)").bitcast(I32),
                )
            return t

        w0_t = load_pair(w0_words, 0, "w0_t")
        load_planes(w0_scales, 0, 2, OFF_W0, N0)
        load_planes(w1_scales, 0, 4, OFF_W1, N1)
        load_planes(w2_scales, 0, 4, OFF_W2A, N2)
        w1_a = load_pair(w1_words, 0, "w1_a")
        w1_b = load_pair(w1_words, 2, "w1_b")
        load_planes(w2_scales, 4, 4, OFF_W2B, N2)
        w2_t = [load_w2(g) for g in range(4)]

        xq = keep.tile([P, K_X // 4], U32, name="xq", align_bytes=256)
        xs = keep.tile([P, K_X // 4], U8, name="xs", align_bytes=256)
        x_words = x_sb[:].bitcast(F32)
        grouped_words = grouped[:].bitcast(F32)
        xt = []
        for b in range(4):
            t = bank("xt%d" % b)
            for gl in range(2):
                g = 2 * b + gl
                for u in range(2):
                    c = (2 * gl + u) * P
                    nc.tensor.transpose(t[:, c:c + P], x_words[:, 256 * g + u:256 * (g + 1):2], ident_f32[:])
            xt.append(t)
        for b in (0, 2, 1, 3):
            dst = grouped_words[:, BANK * b:BANK * (b + 1)].rearrange("p (g m u) -> p g m u", g=2, u=2)
            src = xt[b][:].rearrange("p (g u m) -> p g m u", g=2, u=2)
            if b % 2 == 0:
                nc.vector.tensor_copy(out=dst, in_=src)
            else:
                nc.scalar.copy(out=dst, in_=src)
        for b in range(4):
            nc.vector.quantize_mx(
                out=xq[:, 256 * b:256 * (b + 1)].bitcast(FP8X4),
                scales=xs[:, 256 * b:256 * (b + 1)],
                in_=grouped[:, 1024 * b:1024 * (b + 1)],
            )

        out_sb = keep.tile([P, N_OUT], F32, name="out_sb", align_bytes=256)
        for j in range(n_bias):
            t = bank("bias%d" % j)
            nc.tensor.matmul(
                out=t[:], lhsT=ident_bf[:, j:j + 1].to_broadcast([P, P]), rhs=bias_rows[:], start=True, stop=True
            )
            nc.scalar.copy(out=out_sb[:, BANK * j:BANK * (j + 1)], in_=t[:])

        w2_t.append(load_w2(4))
        w2_t.append(load_w2(5))

        def mx_pass(acc, g, n_groups, words, k_plane, plane_col):
            nc.tensor.matmul_mx(
                out=acc[:],
                lhsT=xq[:, P * g:P * (g + 1)].bitcast(FP8X4),
                lhsT_scale=xs[:, P * g:P * (g + 1)],
                rhs=words.bitcast(FP8X4),
                rhs_scale=planes[k_plane:P, plane_col:plane_col + BANK],
                start=(g == 0),
                stop=(g == n_groups - 1),
            )

        def add_bias(acc, col):
            nc.vector.tensor_tensor(out=out_sb[:, col:col + BANK], in0=acc[:], in1=out_sb[:, col:col + BANK], op=ADD)

        acc0 = [bank("acc0_%d" % j) for j in range(4)]
        for g in range(2):
            for j in range(4):
                mx_pass(acc0[j], g, 2, w0_t[:, g, BANK * j:BANK * (j + 1)], 4 * g, OFF_W0 + BANK * j)
        for j in range(4):
            add_bias(acc0[j], BANK * j)
        w2_t.append(load_w2(6))

        acc1 = [bank("acc1_%d" % j) for j in range(4)]
        for g in range(4):
            src_t = w1_a if g < 2 else w1_b
            for j in range(4):
                mx_pass(acc1[j], g, 4, src_t[:, g % 2, BANK * j:BANK * (j + 1)], 4 * g, OFF_W1 + BANK * j)
        for j in range(4):
            add_bias(acc1[j], N0 + BANK * j)
        w2_t.append(load_w2(7, (0, 2048, 3584, N2)))

        def w2_pass(acc, g, j):
            off = OFF_W2A if g < 4 else OFF_W2B
            mx_pass(acc, g, 8, w2_t[g][:, BANK * j:BANK * (j + 1)], 4 * (g % 4), off + BANK * j)

        acc2 = [bank("acc2_%d" % j) for j in range(8)]
        for g in range(7):
            for j in range(8):
                w2_pass(acc2[j], g, j)
        for j in range(4):
            w2_pass(acc2[j], 7, j)
        for j in range(4):
            add_bias(acc2[j], N0 + N1 + BANK * j)
        for j in range(4, 7):
            w2_pass(acc2[j], 7, j)
        acc_last = bank("acc2_8")
        for g in range(7):
            w2_pass(acc_last, g, 8)
        w2_pass(acc2[7], 7, 7)
        w2_pass(acc_last, 7, 8)
        for j in range(4, 8):
            add_bias(acc2[j], N0 + N1 + BANK * j)
        add_bias(acc_last, N0 + N1 + BANK * 8)

        for lo, hi in ((0, 4096), (4096, 7168), (7168, 8704)):
            nc.sync.dma_start(out=out[:, lo:hi], in_=out_sb[:, lo:hi])
